import numpy as np
import ml_dtypes

BF16 = ml_dtypes.bfloat16


def bf(x):
    return np.asarray(x, np.float32).astype(BF16)


def f32(x):
    return np.asarray(x, np.float32)


def f64(x):
    return np.asarray(x).astype(np.float64)


def striped(idx):
    return np.tile(idx.reshape(-1, 16).T, (8, 1))


S, DEG, HEADS, OUT_F, D, M, N, H, K = 256, 8, 8, 16, 128, 128, 2048, 128, 16
NEG_SLOPE = 0.01


def setup_inputs():
    w_scale = 2.0 * np.sqrt(6.0 / (D + M))
    a_scale = 2.0 * np.sqrt(6.0 / (OUT_F + HEADS))
    q = bf(np.random.standard_normal((D, S)))
    kw = bf((np.random.uniform(size=(D, M)) - 0.5) * w_scale)
    qw = bf((np.random.uniform(size=(D, M)) - 0.5) * w_scale)
    a = (np.random.uniform(size=(M, 1)) - 0.5) * a_scale
    same_head = np.kron(np.eye(HEADS), np.ones((OUT_F, OUT_F)))
    amat = bf(a * same_head)
    idx = np.concatenate([np.random.permutation(S)[:H] for _ in range(K)])
    return {"q": q, "kw": kw, "qw": qw, "amat": amat, "offs": striped(idx)}


def reference(q, kw, qw, amat, offs):
    idx = offs[:16].T.reshape(-1)
    ko = (f64(kw).T @ f64(q)[:, idx]).reshape(M, S, DEG)
    qo = f64(qw).T @ f64(q)
    v = qo[:, :, None] + ko
    x = np.maximum(v, NEG_SLOPE * v)
    z = (f64(amat).T @ x.reshape(M, N)).reshape(M, S, DEG)
    e = np.exp(z - z.max(axis=2, keepdims=True))
    attn = e / e.sum(axis=2, keepdims=True)
    return (attn * ko).sum(axis=2)

@@ -1,0 +1,104 @@
+import concourse.mybir as mybir
+
+F32 = mybir.dt.float32
+BF16 = mybir.dt.bfloat16
+U16 = mybir.dt.uint16
+ALU = mybir.AluOpType
+ACT = mybir.ActivationFunctionType
+X_AXIS = mybir.AxisListType.X
+
+P = 128
+NODES = 256
+DEG = 8
+ENTRIES = NODES * DEG
+PIECE = 128
+BANK = 512
+BANK_NODES = BANK // DEG
+BANKS = ENTRIES // BANK
+NEG_SLOPE = 0.01
+
+FLOPS = 2 * P * P * (ENTRIES + NODES + ENTRIES)
+
+
+def tile_ellgat_kernel(tc, q, kw, qw, amat, offs, out):
+    nc = tc.nc
+    with (
+        tc.tile_pool(name="held", bufs=1) as held,
+        tc.tile_pool(name="work", bufs=2) as work,
+        tc.psum_pool(name="v_banks", bufs=1) as v_banks,
+        tc.psum_pool(name="psum", bufs=2) as psum,
+    ):
+        offsets = held.tile([P, ENTRIES // 16], U16, name="offsets")
+        nc.sync.dma_start(offsets[:], offs)
+        q_sb = held.tile([P, NODES], BF16, name="q_sb")
+        nc.scalar.dma_start(q_sb[:], q)
+        kw_sb = held.tile([P, P], BF16, name="kw_sb")
+        nc.sync.dma_start(kw_sb[:], kw)
+        qw_sb = held.tile([P, P], BF16, name="qw_sb")
+        nc.scalar.dma_start(qw_sb[:], qw)
+        amat_sb = held.tile([P, P], BF16, name="amat_sb")
+        nc.scalar.dma_start(amat_sb[:], amat)
+
+        qo_ps = v_banks.tile([P, NODES], F32, name="qo_ps")
+        nc.tensor.matmul(qo_ps[:], qw_sb[:], q_sb[:], start=True, stop=True)
+        qo_sb = held.tile([P, NODES], F32, name="qo_sb")
+        nc.scalar.activation(qo_sb[:], qo_ps[:], ACT.Copy)
+
+        out_sb = held.tile([P, NODES], F32, name="out_sb")
+
+        v_ps = [v_banks.tile([P, BANK], F32, name=f"v_ps{bank}") for bank in range(BANKS)]
+        for bank in range(BANKS):
+            own = q_sb[:, bank * BANK_NODES : (bank + 1) * BANK_NODES]
+            nc.tensor.matmul(
+                v_ps[bank][:].rearrange("p (n t) -> p n t", t=DEG),
+                qw_sb[:],
+                own.unsqueeze(2).to_broadcast([P, BANK_NODES, DEG]),
+                start=True,
+                stop=False,
+            )
+        for piece in range(ENTRIES // PIECE):
+            bank, part = divmod(piece, BANK // PIECE)
+            nc.tensor.matmul(
+                v_ps[bank][:, part * PIECE : (part + 1) * PIECE],
+                kw_sb[:],
+                q_sb[:].indirect(offsets[:, piece * (PIECE // 16) : (piece + 1) * (PIECE // 16)]),
+                start=False,
+                stop=(part == BANK // PIECE - 1),
+            )
+
+        for bank in range(BANKS):
+            nodes = slice(bank * BANK_NODES, (bank + 1) * BANK_NODES)
+
+            v_sb = work.tile([P, BANK], F32, name="v_sb")
+            nc.scalar.activation(v_sb[:], v_ps[bank][:], ACT.Copy)
+            x_sb = work.tile([P, BANK], BF16, name="x_sb")
+            nc.vector.scalar_tensor_tensor(
+                out=x_sb[:], in0=v_sb[:], scalar=NEG_SLOPE, in1=v_ps[bank][:], op0=ALU.mult, op1=ALU.max
+            )
+
+            z_ps = psum.tile([P, BANK], F32, name="z_ps")
+            nc.tensor.matmul(z_ps[:], amat_sb[:], x_sb[:], start=True, stop=True)
+            z_by_node = z_ps[:].rearrange("p (n t) -> p n t", t=DEG)
+
+            z_max = work.tile([P, BANK_NODES], F32, name="z_max")
+            nc.vector.tensor_reduce(out=z_max[:], in_=z_by_node, axis=X_AXIS, op=ALU.max)
+            e_sb = work.tile([P, BANK_NODES, DEG], F32, name="e_sb")
+            nc.vector.tensor_tensor(
+                e_sb[:], z_by_node, z_max[:].unsqueeze(2).to_broadcast([P, BANK_NODES, DEG]), ALU.subtract
+            )
+            nc.scalar.activation(e_sb[:], e_sb[:], ACT.Exp)
+            e_sum = work.tile([P, BANK_NODES], F32, name="e_sum")
+            nc.vector.tensor_reduce(out=e_sum[:], in_=e_sb[:], axis=X_AXIS, op=ALU.add)
+
+            ev_sb = work.tile([P, BANK_NODES, DEG], F32, name="ev_sb")
+            nc.vector.tensor_tensor(
+                ev_sb[:], e_sb[:], v_sb[:].rearrange("p (n t) -> p n t", t=DEG), ALU.mult
+            )
+            ev_sum = work.tile([P, BANK_NODES], F32, name="ev_sum")
+            nc.vector.tensor_reduce(out=ev_sum[:], in_=ev_sb[:], axis=X_AXIS, op=ALU.add)
+            e_inv = work.tile([P, BANK_NODES], F32, name="e_inv")
+            nc.vector.reciprocal(e_inv[:], e_sum[:])
+            nc.vector.tensor_tensor(ev_sum[:], ev_sum[:], e_inv[:], ALU.mult)
+            nc.vector.tensor_tensor(out_sb[:, nodes], ev_sum[:], qo_sb[:, nodes], ALU.subtract)
+
+        nc.sync.dma_start(out, out_sb[:])

@@ -1,4 +1,5 @@
 import concourse.mybir as mybir
+from concourse.masks import make_identity
 
 F32 = mybir.dt.float32
 BF16 = mybir.dt.bfloat16
@@ -10,11 +11,15 @@ X_AXIS = mybir.AxisListType.X
 P = 128
 NODES = 256
 DEG = 8
+HEADS = 8
+HEAD_F = P // HEADS
 ENTRIES = NODES * DEG
 PIECE = 128
 BANK = 512
 BANK_NODES = BANK // DEG
 BANKS = ENTRIES // BANK
+BLOCKS = NODES // P
+FLIPS = BANK // P
 NEG_SLOPE = 0.01
 
 FLOPS = 2 * P * P * (ENTRIES + NODES + ENTRIES)
@@ -25,8 +30,8 @@ def tile_ellgat_kernel(tc, q, kw, qw, amat, offs, out):
     with (
         tc.tile_pool(name="held", bufs=1) as held,
         tc.tile_pool(name="work", bufs=2) as work,
-        tc.psum_pool(name="v_banks", bufs=1) as v_banks,
-        tc.psum_pool(name="psum", bufs=2) as psum,
+        tc.psum_pool(name="banks", bufs=BANKS) as banks,
+        tc.psum_pool(name="small", bufs=BLOCKS) as small,
     ):
         offsets = held.tile([P, ENTRIES // 16], U16, name="offsets")
         nc.sync.dma_start(offsets[:], offs)
@@ -37,16 +42,18 @@ def tile_ellgat_kernel(tc, q, kw, qw, amat, offs, out):
         qw_sb = held.tile([P, P], BF16, name="qw_sb")
         nc.scalar.dma_start(qw_sb[:], qw)
         amat_sb = held.tile([P, P], BF16, name="amat_sb")
-        nc.scalar.dma_start(amat_sb[:], amat)
+        nc.sync.dma_start(amat_sb[:], amat)
 
-        qo_ps = v_banks.tile([P, NODES], F32, name="qo_ps")
-        nc.tensor.matmul(qo_ps[:], qw_sb[:], q_sb[:], start=True, stop=True)
-        qo_sb = held.tile([P, NODES], F32, name="qo_sb")
-        nc.scalar.activation(qo_sb[:], qo_ps[:], ACT.Copy)
+        ident = held.tile([P, P], F32, name="ident")
+        make_identity(nc, ident[:])
+        first_exp = held.tile([P, 1], F32, name="first_exp")
+        nc.vector.memset(first_exp[:], 0.0)
+        nc.scalar.activation(first_exp[:], first_exp[:], ACT.Exp)
 
-        out_sb = held.tile([P, NODES], F32, name="out_sb")
+        neg_qw = held.tile([P, P], BF16, name="neg_qw")
+        nc.vector.tensor_scalar_mul(neg_qw[:], qw_sb[:], -1.0)
 
-        v_ps = [v_banks.tile([P, BANK], F32, name=f"v_ps{bank}") for bank in range(BANKS)]
+        v_ps = [banks.tile([P, BANK], F32, name=f"v_ps{bank}", tag="bank") for bank in range(BANKS)]
         for bank in range(BANKS):
             own = q_sb[:, bank * BANK_NODES : (bank + 1) * BANK_NODES]
             nc.tensor.matmul(
@@ -66,39 +73,72 @@ def tile_ellgat_kernel(tc, q, kw, qw, amat, offs, out):
                 stop=(part == BANK // PIECE - 1),
             )
 
+        v_sb = held.tile([P, ENTRIES], F32, name="v_sb")
+        x_sb = held.tile([P, ENTRIES], BF16, name="x_sb")
         for bank in range(BANKS):
-            nodes = slice(bank * BANK_NODES, (bank + 1) * BANK_NODES)
-
-            v_sb = work.tile([P, BANK], F32, name="v_sb")
-            nc.scalar.activation(v_sb[:], v_ps[bank][:], ACT.Copy)
-            x_sb = work.tile([P, BANK], BF16, name="x_sb")
+            cols = slice(bank * BANK, (bank + 1) * BANK)
+            nc.scalar.activation(v_sb[:, cols], v_ps[bank][:], ACT.Copy)
             nc.vector.scalar_tensor_tensor(
-                out=x_sb[:], in0=v_sb[:], scalar=NEG_SLOPE, in1=v_ps[bank][:], op0=ALU.mult, op1=ALU.max
+                out=x_sb[:, cols], in0=v_sb[:, cols], scalar=NEG_SLOPE, in1=v_ps[bank][:],
+                op0=ALU.mult, op1=ALU.max,
             )
 
-            z_ps = psum.tile([P, BANK], F32, name="z_ps")
-            nc.tensor.matmul(z_ps[:], amat_sb[:], x_sb[:], start=True, stop=True)
-            z_by_node = z_ps[:].rearrange("p (n t) -> p n t", t=DEG)
+        x_by_t = x_sb[:].rearrange("p (b n t) -> p b t n", b=BLOCKS, t=DEG)
+        v_by_t = v_sb[:].rearrange("p (b n t) -> p b t n", b=BLOCKS, t=DEG)
+        amat_heads = amat_sb[:].rearrange("p (h o) -> p o h", o=HEAD_F)[:, 0, :]
 
-            z_max = work.tile([P, BANK_NODES], F32, name="z_max")
-            nc.vector.tensor_reduce(out=z_max[:], in_=z_by_node, axis=X_AXIS, op=ALU.max)
-            e_sb = work.tile([P, BANK_NODES, DEG], F32, name="e_sb")
+        attn = []
+        v_flipped = []
+        for block in range(BLOCKS):
+            z_ps = small.tile([P, DEG, HEADS], F32, name="z_ps")
+            for t in range(DEG):
+                nc.tensor.matmul(z_ps[:, t, :], x_by_t[:, block, t, :], amat_heads, start=True, stop=True)
+
+            z_max = work.tile([P, HEADS], F32, name="z_max")
+            nc.vector.tensor_reduce(
+                out=z_max[:], in_=z_ps[:].rearrange("p t h -> p h t"), axis=X_AXIS, op=ALU.max
+            )
+            e_sb = work.tile([P, DEG, HEADS], F32, name="e_sb")
             nc.vector.tensor_tensor(
-                e_sb[:], z_by_node, z_max[:].unsqueeze(2).to_broadcast([P, BANK_NODES, DEG]), ALU.subtract
+                e_sb[:], z_ps[:], z_max[:].unsqueeze(1).to_broadcast([P, DEG, HEADS]), ALU.subtract
             )
             nc.scalar.activation(e_sb[:], e_sb[:], ACT.Exp)
-            e_sum = work.tile([P, BANK_NODES], F32, name="e_sum")
-            nc.vector.tensor_reduce(out=e_sum[:], in_=e_sb[:], axis=X_AXIS, op=ALU.add)
-
-            ev_sb = work.tile([P, BANK_NODES, DEG], F32, name="ev_sb")
-            nc.vector.tensor_tensor(
-                ev_sb[:], e_sb[:], v_sb[:].rearrange("p (n t) -> p n t", t=DEG), ALU.mult
+            e_sum = work.tile([P, HEADS], F32, name="e_sum")
+            nc.vector.tensor_reduce(
+                out=e_sum[:], in_=e_sb[:].rearrange("p t h -> p h t"), axis=X_AXIS, op=ALU.add
             )
-            ev_sum = work.tile([P, BANK_NODES], F32, name="ev_sum")
-            nc.vector.tensor_reduce(out=ev_sum[:], in_=ev_sb[:], axis=X_AXIS, op=ALU.add)
-            e_inv = work.tile([P, BANK_NODES], F32, name="e_inv")
+            e_inv = work.tile([P, HEADS], F32, name="e_inv")
             nc.vector.reciprocal(e_inv[:], e_sum[:])
-            nc.vector.tensor_tensor(ev_sum[:], ev_sum[:], e_inv[:], ALU.mult)
-            nc.vector.tensor_tensor(out_sb[:, nodes], ev_sum[:], qo_sb[:, nodes], ALU.subtract)
+            attn_sb = work.tile([P, DEG, HEADS], F32, name="attn_sb")
+            nc.vector.tensor_tensor(
+                attn_sb[:], e_sb[:], e_inv[:].unsqueeze(1).to_broadcast([P, DEG, HEADS]), ALU.mult
+            )
+            attn.append(attn_sb)
 
-        nc.sync.dma_start(out, out_sb[:])
+            for group in range(DEG // FLIPS):
+                vt_ps = banks.tile([P, FLIPS, P], F32, name=f"vt_ps{block}{group}", tag="bank")
+                for k in range(FLIPS):
+                    nc.tensor.transpose(vt_ps[:, k, :], v_by_t[:, block, group * FLIPS + k, :], ident[:])
+                v_flipped.append(vt_ps)
+
+        for block in range(BLOCKS):
+            nodes = slice(block * P, (block + 1) * P)
+            out_ps = small.tile([P, P], F32, name="out_ps")
+            nc.tensor.matmul(out_ps[:], neg_qw[:], q_sb[:, nodes], start=True, stop=False)
+            for group in range(DEG // FLIPS):
+                ts = slice(group * FLIPS, (group + 1) * FLIPS)
+                av_sb = work.tile([P, FLIPS, P], F32, name="av_sb")
+                nc.vector.tensor_tensor(
+                    av_sb[:].rearrange("p k (h o) -> p k h o", o=HEAD_F),
+                    v_flipped[block * (DEG // FLIPS) + group][:].rearrange("p k (h o) -> p k h o", o=HEAD_F),
+                    attn[block][:, ts, :].unsqueeze(3).to_broadcast([P, FLIPS, HEADS, HEAD_F]),
+                    ALU.mult,
+                )
+                for k in range(FLIPS):
+                    nc.tensor.matmul(
+                        out_ps[:], av_sb[:, k, :], ident[:], is_transpose=True,
+                        start=False, stop=(group * FLIPS + k == DEG - 1),
+                    )
+            out_sb = work.tile([P, P], F32, name="out_sb")
+            nc.scalar.activation(out_sb[:], out_ps[:], ACT.Copy)
+            nc.sync.dma_start(out[:, nodes], out_sb[:])

@@ -14,13 +14,14 @@ DEG = 8
 HEADS = 8
 HEAD_F = P // HEADS
 ENTRIES = NODES * DEG
-PIECE = 128
 BANK = 512
 BANK_NODES = BANK // DEG
 BANKS = ENTRIES // BANK
 BLOCKS = NODES // P
 FLIPS = BANK // P
+PIECES = (128, 128, 256)
 NEG_SLOPE = 0.01
+WARM_UPS = 3
 
 FLOPS = 2 * P * P * (ENTRIES + NODES + ENTRIES)
 
@@ -54,6 +55,12 @@ def tile_ellgat_kernel(tc, q, kw, qw, amat, offs, out):
         nc.vector.tensor_scalar_mul(neg_qw[:], qw_sb[:], -1.0)
 
         v_ps = [banks.tile([P, BANK], F32, name=f"v_ps{bank}", tag="bank") for bank in range(BANKS)]
+
+        zeros = held.tile([P, BANK], BF16, name="zeros")
+        nc.vector.memset(zeros[:], 0.0)
+        for rep in range(WARM_UPS):
+            nc.tensor.matmul(v_ps[BANKS - 1][:], zeros[:, 0:P], zeros[:], start=True, stop=True)
+
         for bank in range(BANKS):
             own = q_sb[:, bank * BANK_NODES : (bank + 1) * BANK_NODES]
             nc.tensor.matmul(
@@ -63,15 +70,18 @@ def tile_ellgat_kernel(tc, q, kw, qw, amat, offs, out):
                 start=True,
                 stop=False,
             )
-        for piece in range(ENTRIES // PIECE):
-            bank, part = divmod(piece, BANK // PIECE)
-            nc.tensor.matmul(
-                v_ps[bank][:, part * PIECE : (part + 1) * PIECE],
-                kw_sb[:],
-                q_sb[:].indirect(offsets[:, piece * (PIECE // 16) : (piece + 1) * (PIECE // 16)]),
-                start=False,
-                stop=(part == BANK // PIECE - 1),
-            )
+        for bank in range(BANKS):
+            first = 0
+            for width in PIECES:
+                entry = bank * BANK + first
+                nc.tensor.matmul(
+                    v_ps[bank][:, first : first + width],
+                    kw_sb[:],
+                    q_sb[:].indirect(offsets[:, entry // 16 : (entry + width) // 16]),
+                    start=False,
+                    stop=(first + width == BANK),
+                )
+                first += width
 
         v_sb = held.tile([P, ENTRIES], F32, name="v_sb")
         x_sb = held.tile([P, ENTRIES], BF16, name="x_sb")
@@ -87,20 +97,22 @@ def tile_ellgat_kernel(tc, q, kw, qw, amat, offs, out):
         v_by_t = v_sb[:].rearrange("p (b n t) -> p b t n", b=BLOCKS, t=DEG)
         amat_heads = amat_sb[:].rearrange("p (h o) -> p o h", o=HEAD_F)[:, 0, :]
 
-        attn = []
-        v_flipped = []
+        z_ps = [small.tile([P, DEG, HEADS], F32, name=f"z_ps{block}", tag="z_ps") for block in range(BLOCKS)]
         for block in range(BLOCKS):
-            z_ps = small.tile([P, DEG, HEADS], F32, name="z_ps")
             for t in range(DEG):
-                nc.tensor.matmul(z_ps[:, t, :], x_by_t[:, block, t, :], amat_heads, start=True, stop=True)
+                nc.tensor.matmul(
+                    z_ps[block][:, t, :], x_by_t[:, block, t, :], amat_heads, start=True, stop=True
+                )
 
+        attn = []
+        for block in range(BLOCKS):
             z_max = work.tile([P, HEADS], F32, name="z_max")
             nc.vector.tensor_reduce(
-                out=z_max[:], in_=z_ps[:].rearrange("p t h -> p h t"), axis=X_AXIS, op=ALU.max
+                out=z_max[:], in_=z_ps[block][:].rearrange("p t h -> p h t"), axis=X_AXIS, op=ALU.max
             )
             e_sb = work.tile([P, DEG, HEADS], F32, name="e_sb")
             nc.vector.tensor_tensor(
-                e_sb[:], z_ps[:], z_max[:].unsqueeze(1).to_broadcast([P, DEG, HEADS]), ALU.subtract
+                e_sb[:], z_ps[block][:], z_max[:].unsqueeze(1).to_broadcast([P, DEG, HEADS]), ALU.subtract
             )
             nc.scalar.activation(e_sb[:], e_sb[:], ACT.Exp)
             e_sum = work.tile([P, HEADS], F32, name="e_sum")
@@ -115,6 +127,8 @@ def tile_ellgat_kernel(tc, q, kw, qw, amat, offs, out):
             )
             attn.append(attn_sb)
 
+        v_flipped = []
+        for block in range(BLOCKS):
             for group in range(DEG // FLIPS):
                 vt_ps = banks.tile([P, FLIPS, P], F32, name=f"vt_ps{block}{group}", tag="bank")
                 for k in range(FLIPS):

@@ -18,6 +18,7 @@ BANK = 512
 BANK_NODES = BANK // DEG
 BANKS = ENTRIES // BANK
 BLOCKS = NODES // P
+BLOCK_BANKS = BANKS // BLOCKS
 FLIPS = BANK // P
 PIECES = (128, 128, 256)
 NEG_SLOPE = 0.01
@@ -45,6 +46,12 @@ def tile_ellgat_kernel(tc, q, kw, qw, amat, offs, out):
         amat_sb = held.tile([P, P], BF16, name="amat_sb")
         nc.sync.dma_start(amat_sb[:], amat)
 
+        v_ps = [banks.tile([P, BANK_NODES, DEG], F32, name=f"v_ps{bank}", tag="bank") for bank in range(BANKS)]
+
+        zeros = held.tile([P, BANK], BF16, name="zeros")
+        nc.vector.memset(zeros[:], 0.0)
+        for rep in range(WARM_UPS):
+            nc.tensor.matmul(v_ps[BANKS - 1][:], zeros[:, 0:P], zeros[:], start=True, stop=True)
         ident = held.tile([P, P], F32, name="ident")
         make_identity(nc, ident[:])
         first_exp = held.tile([P, 1], F32, name="first_exp")
@@ -54,28 +61,18 @@ def tile_ellgat_kernel(tc, q, kw, qw, amat, offs, out):
         neg_qw = held.tile([P, P], BF16, name="neg_qw")
         nc.vector.tensor_scalar_mul(neg_qw[:], qw_sb[:], -1.0)
 
-        v_ps = [banks.tile([P, BANK], F32, name=f"v_ps{bank}", tag="bank") for bank in range(BANKS)]
-
-        zeros = held.tile([P, BANK], BF16, name="zeros")
-        nc.vector.memset(zeros[:], 0.0)
-        for rep in range(WARM_UPS):
-            nc.tensor.matmul(v_ps[BANKS - 1][:], zeros[:, 0:P], zeros[:], start=True, stop=True)
-
         for bank in range(BANKS):
             own = q_sb[:, bank * BANK_NODES : (bank + 1) * BANK_NODES]
             nc.tensor.matmul(
-                v_ps[bank][:].rearrange("p (n t) -> p n t", t=DEG),
-                qw_sb[:],
-                own.unsqueeze(2).to_broadcast([P, BANK_NODES, DEG]),
-                start=True,
-                stop=False,
+                v_ps[bank][:], qw_sb[:], own.unsqueeze(2).to_broadcast([P, BANK_NODES, DEG]),
+                start=True, stop=False,
             )
         for bank in range(BANKS):
             first = 0
             for width in PIECES:
                 entry = bank * BANK + first
                 nc.tensor.matmul(
-                    v_ps[bank][:, first : first + width],
+                    v_ps[bank][:, first // DEG : (first + width) // DEG, :],
                     kw_sb[:],
                     q_sb[:].indirect(offsets[:, entry // 16 : (entry + width) // 16]),
                     start=False,
@@ -83,26 +80,25 @@ def tile_ellgat_kernel(tc, q, kw, qw, amat, offs, out):
                 )
                 first += width
 
-        v_sb = held.tile([P, ENTRIES], F32, name="v_sb")
-        x_sb = held.tile([P, ENTRIES], BF16, name="x_sb")
+        v_sb = held.tile([P, BLOCKS, DEG, P], F32, name="v_sb")
+        x_sb = held.tile([P, BLOCKS, DEG, P], BF16, name="x_sb")
         for bank in range(BANKS):
-            cols = slice(bank * BANK, (bank + 1) * BANK)
-            nc.scalar.activation(v_sb[:, cols], v_ps[bank][:], ACT.Copy)
-            nc.vector.scalar_tensor_tensor(
-                out=x_sb[:, cols], in0=v_sb[:, cols], scalar=NEG_SLOPE, in1=v_ps[bank][:],
-                op0=ALU.mult, op1=ALU.max,
-            )
+            block, side = divmod(bank, BLOCK_BANKS)
+            cols = slice(side * BANK_NODES, (side + 1) * BANK_NODES)
+            for ts in (slice(0, DEG // 2), slice(DEG // 2, DEG)):
+                nc.scalar.activation(
+                    v_sb[:, block, ts, cols].rearrange("p t n -> p n t"), v_ps[bank][:, :, ts], ACT.Copy
+                )
+                nc.vector.scalar_tensor_tensor(
+                    out=x_sb[:, block, ts, cols], in0=v_sb[:, block, ts, cols], scalar=NEG_SLOPE,
+                    in1=v_sb[:, block, ts, cols], op0=ALU.mult, op1=ALU.max,
+                )
 
-        x_by_t = x_sb[:].rearrange("p (b n t) -> p b t n", b=BLOCKS, t=DEG)
-        v_by_t = v_sb[:].rearrange("p (b n t) -> p b t n", b=BLOCKS, t=DEG)
         amat_heads = amat_sb[:].rearrange("p (h o) -> p o h", o=HEAD_F)[:, 0, :]
-
         z_ps = [small.tile([P, DEG, HEADS], F32, name=f"z_ps{block}", tag="z_ps") for block in range(BLOCKS)]
         for block in range(BLOCKS):
             for t in range(DEG):
-                nc.tensor.matmul(
-                    z_ps[block][:, t, :], x_by_t[:, block, t, :], amat_heads, start=True, stop=True
-                )
+                nc.tensor.matmul(z_ps[block][:, t, :], x_sb[:, block, t, :], amat_heads, start=True, stop=True)
 
         attn = []
         for block in range(BLOCKS):
@@ -132,9 +128,10 @@ def tile_ellgat_kernel(tc, q, kw, qw, amat, offs, out):
             for group in range(DEG // FLIPS):
                 vt_ps = banks.tile([P, FLIPS, P], F32, name=f"vt_ps{block}{group}", tag="bank")
                 for k in range(FLIPS):
-                    nc.tensor.transpose(vt_ps[:, k, :], v_by_t[:, block, group * FLIPS + k, :], ident[:])
+                    nc.tensor.transpose(vt_ps[:, k, :], v_sb[:, block, group * FLIPS + k, :], ident[:])
                 v_flipped.append(vt_ps)
 
+        out_queues = (nc.sync, nc.scalar)
         for block in range(BLOCKS):
             nodes = slice(block * P, (block + 1) * P)
             out_ps = small.tile([P, P], F32, name="out_ps")
@@ -154,5 +151,5 @@ def tile_ellgat_kernel(tc, q, kw, qw, amat, offs, out):
                         start=False, stop=(group * FLIPS + k == DEG - 1),
                     )
             out_sb = work.tile([P, P], F32, name="out_sb")
-            nc.scalar.activation(out_sb[:], out_ps[:], ACT.Copy)
-            nc.sync.dma_start(out[:, nodes], out_sb[:])
+            nc.vector.tensor_copy(out_sb[:], out_ps[:])
+            out_queues[block].dma_start(out[:, nodes], out_sb[:])

@@ -20,9 +20,8 @@ BANKS = ENTRIES // BANK
 BLOCKS = NODES // P
 BLOCK_BANKS = BANKS // BLOCKS
 FLIPS = BANK // P
-PIECES = (128, 128, 256)
+PIECE = 128
 NEG_SLOPE = 0.01
-WARM_UPS = 3
 
 FLOPS = 2 * P * P * (ENTRIES + NODES + ENTRIES)
 
@@ -48,10 +47,6 @@ def tile_ellgat_kernel(tc, q, kw, qw, amat, offs, out):
 
         v_ps = [banks.tile([P, BANK_NODES, DEG], F32, name=f"v_ps{bank}", tag="bank") for bank in range(BANKS)]
 
-        zeros = held.tile([P, BANK], BF16, name="zeros")
-        nc.vector.memset(zeros[:], 0.0)
-        for rep in range(WARM_UPS):
-            nc.tensor.matmul(v_ps[BANKS - 1][:], zeros[:, 0:P], zeros[:], start=True, stop=True)
         ident = held.tile([P, P], F32, name="ident")
         make_identity(nc, ident[:])
         first_exp = held.tile([P, 1], F32, name="first_exp")
@@ -67,18 +62,15 @@ def tile_ellgat_kernel(tc, q, kw, qw, amat, offs, out):
                 v_ps[bank][:], qw_sb[:], own.unsqueeze(2).to_broadcast([P, BANK_NODES, DEG]),
                 start=True, stop=False,
             )
-        for bank in range(BANKS):
-            first = 0
-            for width in PIECES:
-                entry = bank * BANK + first
-                nc.tensor.matmul(
-                    v_ps[bank][:, first // DEG : (first + width) // DEG, :],
-                    kw_sb[:],
-                    q_sb[:].indirect(offsets[:, entry // 16 : (entry + width) // 16]),
-                    start=False,
-                    stop=(first + width == BANK),
-                )
-                first += width
+        for piece in range(ENTRIES // PIECE):
+            bank, part = divmod(piece, BANK // PIECE)
+            nc.tensor.matmul(
+                v_ps[bank][:, part * (PIECE // DEG) : (part + 1) * (PIECE // DEG), :],
+                kw_sb[:],
+                q_sb[:].indirect(offsets[:, piece * (PIECE // 16) : (piece + 1) * (PIECE // 16)]),
+                start=False,
+                stop=(part == BANK // PIECE - 1),
+            )
 
         v_sb = held.tile([P, BLOCKS, DEG, P], F32, name="v_sb")
         x_sb = held.tile([P, BLOCKS, DEG, P], BF16, name="x_sb")

@@ -20,8 +20,9 @@ BANKS = ENTRIES // BANK
 BLOCKS = NODES // P
 BLOCK_BANKS = BANKS // BLOCKS
 FLIPS = BANK // P
-PIECE = 128
+PIECES = (128, 128, 256)
 NEG_SLOPE = 0.01
+WARM_UPS = 3
 
 FLOPS = 2 * P * P * (ENTRIES + NODES + ENTRIES)
 
@@ -47,6 +48,10 @@ def tile_ellgat_kernel(tc, q, kw, qw, amat, offs, out):
 
         v_ps = [banks.tile([P, BANK_NODES, DEG], F32, name=f"v_ps{bank}", tag="bank") for bank in range(BANKS)]
 
+        zeros = held.tile([P, BANK], BF16, name="zeros")
+        nc.vector.memset(zeros[:], 0.0)
+        for rep in range(WARM_UPS):
+            nc.tensor.matmul(v_ps[BANKS - 1][:], zeros[:, 0:P], zeros[:], start=True, stop=True)
         ident = held.tile([P, P], F32, name="ident")
         make_identity(nc, ident[:])
         first_exp = held.tile([P, 1], F32, name="first_exp")
@@ -62,15 +67,18 @@ def tile_ellgat_kernel(tc, q, kw, qw, amat, offs, out):
                 v_ps[bank][:], qw_sb[:], own.unsqueeze(2).to_broadcast([P, BANK_NODES, DEG]),
                 start=True, stop=False,
             )
-        for piece in range(ENTRIES // PIECE):
-            bank, part = divmod(piece, BANK // PIECE)
-            nc.tensor.matmul(
-                v_ps[bank][:, part * (PIECE // DEG) : (part + 1) * (PIECE // DEG), :],
-                kw_sb[:],
-                q_sb[:].indirect(offsets[:, piece * (PIECE // 16) : (piece + 1) * (PIECE // 16)]),
-                start=False,
-                stop=(part == BANK // PIECE - 1),
-            )
+        for bank in range(BANKS):
+            first = 0
+            for width in PIECES:
+                entry = bank * BANK + first
+                nc.tensor.matmul(
+                    v_ps[bank][:, first // DEG : (first + width) // DEG, :],
+                    kw_sb[:],
+                    q_sb[:].indirect(offsets[:, entry // 16 : (entry + width) // 16]),
+                    start=False,
+                    stop=(first + width == BANK),
+                )
+                first += width
 
         v_sb = held.tile([P, BLOCKS, DEG, P], F32, name="v_sb")
         x_sb = held.tile([P, BLOCKS, DEG, P], BF16, name="x_sb")
@@ -126,22 +134,25 @@ def tile_ellgat_kernel(tc, q, kw, qw, amat, offs, out):
         out_queues = (nc.sync, nc.scalar)
         for block in range(BLOCKS):
             nodes = slice(block * P, (block + 1) * P)
-            out_ps = small.tile([P, P], F32, name="out_ps")
-            nc.tensor.matmul(out_ps[:], neg_qw[:], q_sb[:, nodes], start=True, stop=False)
+            products = []
             for group in range(DEG // FLIPS):
                 ts = slice(group * FLIPS, (group + 1) * FLIPS)
-                av_sb = work.tile([P, FLIPS, P], F32, name="av_sb")
+                av_sb = work.tile([P, FLIPS, P], F32, name="av_sb", bufs=BANKS)
                 nc.vector.tensor_tensor(
                     av_sb[:].rearrange("p k (h o) -> p k h o", o=HEAD_F),
                     v_flipped[block * (DEG // FLIPS) + group][:].rearrange("p k (h o) -> p k h o", o=HEAD_F),
                     attn[block][:, ts, :].unsqueeze(3).to_broadcast([P, FLIPS, HEADS, HEAD_F]),
                     ALU.mult,
                 )
-                for k in range(FLIPS):
-                    nc.tensor.matmul(
-                        out_ps[:], av_sb[:, k, :], ident[:], is_transpose=True,
-                        start=False, stop=(group * FLIPS + k == DEG - 1),
-                    )
+                products.append(av_sb)
+            nc.vector.tensor_tensor(products[0][:], products[0][:], products[1][:], ALU.add)
+            out_ps = small.tile([P, P], F32, name="out_ps")
+            nc.tensor.matmul(out_ps[:], neg_qw[:], q_sb[:, nodes], start=True, stop=False)
+            for k in range(FLIPS):
+                nc.tensor.matmul(
+                    out_ps[:], products[0][:, k, :], ident[:], is_transpose=True,
+                    start=False, stop=(k == FLIPS - 1),
+                )
             out_sb = work.tile([P, P], F32, name="out_sb")
             nc.vector.tensor_copy(out_sb[:], out_ps[:])
             out_queues[block].dma_start(out[:, nodes], out_sb[:])

@@ -100,28 +100,17 @@ def tile_ellgat_kernel(tc, q, kw, qw, amat, offs, out):
             for t in range(DEG):
                 nc.tensor.matmul(z_ps[block][:, t, :], x_sb[:, block, t, :], amat_heads, start=True, stop=True)
 
-        attn = []
+        e_sb = [held.tile([P, DEG, HEADS], F32, name=f"e_sb{block}") for block in range(BLOCKS)]
         for block in range(BLOCKS):
             z_max = work.tile([P, HEADS], F32, name="z_max")
             nc.vector.tensor_reduce(
                 out=z_max[:], in_=z_ps[block][:].rearrange("p t h -> p h t"), axis=X_AXIS, op=ALU.max
             )
-            e_sb = work.tile([P, DEG, HEADS], F32, name="e_sb")
             nc.vector.tensor_tensor(
-                e_sb[:], z_ps[block][:], z_max[:].unsqueeze(1).to_broadcast([P, DEG, HEADS]), ALU.subtract
+                e_sb[block][:], z_ps[block][:], z_max[:].unsqueeze(1).to_broadcast([P, DEG, HEADS]),
+                ALU.subtract,
             )
-            nc.scalar.activation(e_sb[:], e_sb[:], ACT.Exp)
-            e_sum = work.tile([P, HEADS], F32, name="e_sum")
-            nc.vector.tensor_reduce(
-                out=e_sum[:], in_=e_sb[:].rearrange("p t h -> p h t"), axis=X_AXIS, op=ALU.add
-            )
-            e_inv = work.tile([P, HEADS], F32, name="e_inv")
-            nc.vector.reciprocal(e_inv[:], e_sum[:])
-            attn_sb = work.tile([P, DEG, HEADS], F32, name="attn_sb")
-            nc.vector.tensor_tensor(
-                attn_sb[:], e_sb[:], e_inv[:].unsqueeze(1).to_broadcast([P, DEG, HEADS]), ALU.mult
-            )
-            attn.append(attn_sb)
+            nc.scalar.activation(e_sb[block][:], e_sb[block][:], ACT.Exp)
 
         v_flipped = []
         for block in range(BLOCKS):
@@ -131,28 +120,39 @@ def tile_ellgat_kernel(tc, q, kw, qw, amat, offs, out):
                     nc.tensor.transpose(vt_ps[:, k, :], v_sb[:, block, group * FLIPS + k, :], ident[:])
                 v_flipped.append(vt_ps)
 
-        out_queues = (nc.sync, nc.scalar)
+        out_ps = [small.tile([P, P], F32, name=f"out_ps{block}", tag="out_ps") for block in range(BLOCKS)]
         for block in range(BLOCKS):
-            nodes = slice(block * P, (block + 1) * P)
-            products = []
+            e_sum = work.tile([P, HEADS], F32, name="e_sum")
+            nc.vector.tensor_reduce(
+                out=e_sum[:], in_=e_sb[block][:].rearrange("p t h -> p h t"), axis=X_AXIS, op=ALU.add
+            )
+            e_inv = work.tile([P, HEADS], F32, name="e_inv")
+            nc.vector.reciprocal(e_inv[:], e_sum[:])
+            attn_sb = work.tile([P, DEG, HEADS], F32, name="attn_sb")
+            nc.vector.tensor_tensor(
+                attn_sb[:], e_sb[block][:], e_inv[:].unsqueeze(1).to_broadcast([P, DEG, HEADS]), ALU.mult
+            )
+
+            nc.tensor.matmul(
+                out_ps[block][:], neg_qw[:], q_sb[:, block * P : (block + 1) * P], start=True, stop=False
+            )
             for group in range(DEG // FLIPS):
                 ts = slice(group * FLIPS, (group + 1) * FLIPS)
                 av_sb = work.tile([P, FLIPS, P], F32, name="av_sb", bufs=BANKS)
                 nc.vector.tensor_tensor(
                     av_sb[:].rearrange("p k (h o) -> p k h o", o=HEAD_F),
                     v_flipped[block * (DEG // FLIPS) + group][:].rearrange("p k (h o) -> p k h o", o=HEAD_F),
-                    attn[block][:, ts, :].unsqueeze(3).to_broadcast([P, FLIPS, HEADS, HEAD_F]),
+                    attn_sb[:, ts, :].unsqueeze(3).to_broadcast([P, FLIPS, HEADS, HEAD_F]),
                     ALU.mult,
                 )
-                products.append(av_sb)
-            nc.vector.tensor_tensor(products[0][:], products[0][:], products[1][:], ALU.add)
-            out_ps = small.tile([P, P], F32, name="out_ps")
-            nc.tensor.matmul(out_ps[:], neg_qw[:], q_sb[:, nodes], start=True, stop=False)
-            for k in range(FLIPS):
-                nc.tensor.matmul(
-                    out_ps[:], products[0][:, k, :], ident[:], is_transpose=True,
-                    start=False, stop=(k == FLIPS - 1),
-                )
+                for k in range(FLIPS):
+                    nc.tensor.matmul(
+                        out_ps[block][:], av_sb[:, k, :], ident[:], is_transpose=True,
+                        start=False, stop=(group * FLIPS + k == DEG - 1),
+                    )
+
+        out_queues = (nc.sync, nc.scalar)
+        for block in range(BLOCKS):
             out_sb = work.tile([P, P], F32, name="out_sb")
-            nc.vector.tensor_copy(out_sb[:], out_ps[:])
-            out_queues[block].dma_start(out[:, nodes], out_sb[:])
+            nc.vector.tensor_copy(out_sb[:], out_ps[block][:])
+            out_queues[block].dma_start(out[:, block * P : (block + 1) * P], out_sb[:])

@@ -95,64 +95,77 @@ def tile_ellgat_kernel(tc, q, kw, qw, amat, offs, out):
                 )
 
         amat_heads = amat_sb[:].rearrange("p (h o) -> p o h", o=HEAD_F)[:, 0, :]
-        z_ps = [small.tile([P, DEG, HEADS], F32, name=f"z_ps{block}", tag="z_ps") for block in range(BLOCKS)]
+        z_ps = [small.tile([P, P], F32, name=f"z_ps{block}", tag="z_ps") for block in range(BLOCKS)]
         for block in range(BLOCKS):
             for t in range(DEG):
-                nc.tensor.matmul(z_ps[block][:, t, :], x_sb[:, block, t, :], amat_heads, start=True, stop=True)
+                nc.tensor.matmul(
+                    z_ps[block][:, t * HEADS : (t + 1) * HEADS], x_sb[:, block, t, :], amat_heads, start=True, stop=True
+                )
 
         e_sb = [held.tile([P, DEG, HEADS], F32, name=f"e_sb{block}") for block in range(BLOCKS)]
         for block in range(BLOCKS):
             z_max = work.tile([P, HEADS], F32, name="z_max")
             nc.vector.tensor_reduce(
-                out=z_max[:], in_=z_ps[block][:].rearrange("p t h -> p h t"), axis=X_AXIS, op=ALU.max
+                out=z_max[:], in_=z_ps[block][:, 0:DEG * HEADS].rearrange("p (t h) -> p h t", h=HEADS),
+                axis=X_AXIS, op=ALU.max,
             )
             nc.vector.tensor_tensor(
-                e_sb[block][:], z_ps[block][:], z_max[:].unsqueeze(1).to_broadcast([P, DEG, HEADS]),
-                ALU.subtract,
+                e_sb[block][:], z_ps[block][:, 0:DEG * HEADS].rearrange("p (t h) -> p t h", h=HEADS),
+                z_max[:].unsqueeze(1).to_broadcast([P, DEG, HEADS]), ALU.subtract,
             )
             nc.scalar.activation(e_sb[block][:], e_sb[block][:], ACT.Exp)
 
-        v_flipped = []
+        ko_flipped = []
         for block in range(BLOCKS):
             for group in range(DEG // FLIPS):
-                vt_ps = banks.tile([P, FLIPS, P], F32, name=f"vt_ps{block}{group}", tag="bank")
+                kt_ps = banks.tile([P, FLIPS, P], F32, name=f"kt_ps{block}{group}", tag="bank")
                 for k in range(FLIPS):
-                    nc.tensor.transpose(vt_ps[:, k, :], v_sb[:, block, group * FLIPS + k, :], ident[:])
-                v_flipped.append(vt_ps)
+                    nc.tensor.matmul(
+                        kt_ps[:, k, :], v_sb[:, block, group * FLIPS + k, :], ident[:], is_transpose=True,
+                        start=(k == 0), stop=False,
+                    )
+                nc.tensor.matmul(
+                    kt_ps[:], q_sb[:, block * P : (block + 1) * P],
+                    neg_qw[:].unsqueeze(1).to_broadcast([P, FLIPS, P]), start=False, stop=True,
+                )
+                ko_flipped.append(kt_ps)
 
         out_ps = [small.tile([P, P], F32, name=f"out_ps{block}", tag="out_ps") for block in range(BLOCKS)]
+        inv_flipped = []
         for block in range(BLOCKS):
             e_sum = work.tile([P, HEADS], F32, name="e_sum")
             nc.vector.tensor_reduce(
                 out=e_sum[:], in_=e_sb[block][:].rearrange("p t h -> p h t"), axis=X_AXIS, op=ALU.add
             )
             e_inv = work.tile([P, HEADS], F32, name="e_inv")
-            nc.vector.reciprocal(e_inv[:], e_sum[:])
-            attn_sb = work.tile([P, DEG, HEADS], F32, name="attn_sb")
-            nc.vector.tensor_tensor(
-                attn_sb[:], e_sb[block][:], e_inv[:].unsqueeze(1).to_broadcast([P, DEG, HEADS]), ALU.mult
-            )
-
-            nc.tensor.matmul(
-                out_ps[block][:], neg_qw[:], q_sb[:, block * P : (block + 1) * P], start=True, stop=False
-            )
             for group in range(DEG // FLIPS):
                 ts = slice(group * FLIPS, (group + 1) * FLIPS)
-                av_sb = work.tile([P, FLIPS, P], F32, name="av_sb", bufs=BANKS)
+                ek_sb = work.tile([P, FLIPS, P], F32, name="ek_sb", bufs=BANKS)
                 nc.vector.tensor_tensor(
-                    av_sb[:].rearrange("p k (h o) -> p k h o", o=HEAD_F),
-                    v_flipped[block * (DEG // FLIPS) + group][:].rearrange("p k (h o) -> p k h o", o=HEAD_F),
-                    attn_sb[:, ts, :].unsqueeze(3).to_broadcast([P, FLIPS, HEADS, HEAD_F]),
+                    ek_sb[:].rearrange("p k (h o) -> p k h o", o=HEAD_F),
+                    ko_flipped[block * (DEG // FLIPS) + group][:].rearrange("p k (h o) -> p k h o", o=HEAD_F),
+                    e_sb[block][:, ts, :].unsqueeze(3).to_broadcast([P, FLIPS, HEADS, HEAD_F]),
                     ALU.mult,
                 )
                 for k in range(FLIPS):
                     nc.tensor.matmul(
-                        out_ps[block][:], av_sb[:, k, :], ident[:], is_transpose=True,
-                        start=False, stop=(group * FLIPS + k == DEG - 1),
+                        out_ps[block][:], ek_sb[:, k, :], ident[:], is_transpose=True,
+                        start=(group * FLIPS + k == 0), stop=(group * FLIPS + k == DEG - 1),
                     )
+                if group == 0:
+                    nc.vector.reciprocal(e_inv[:], e_sum[:])
+                    inv_wide = work.tile([P, HEADS, HEAD_F], F32, name="inv_wide")
+                    nc.scalar.activation(
+                        inv_wide[:], e_inv[:].unsqueeze(2).to_broadcast([P, HEADS, HEAD_F]), ACT.Copy
+                    )
+                    inv_ps = small.tile([P, P], F32, name=f"inv_ps{block}", tag="z_ps")
+                    nc.tensor.transpose(inv_ps[:], inv_wide[:].rearrange("p h o -> p (h o)"), ident[:])
+                    inv_sb = work.tile([P, P], F32, name="inv_sb")
+                    nc.scalar.activation(inv_sb[:], inv_ps[:], ACT.Copy)
+                    inv_flipped.append(inv_sb)
 
         out_queues = (nc.sync, nc.scalar)
         for block in range(BLOCKS):
             out_sb = work.tile([P, P], F32, name="out_sb")
-            nc.vector.tensor_copy(out_sb[:], out_ps[block][:])
+            nc.vector.tensor_tensor(out_sb[:], out_ps[block][:], inv_flipped[block][:], ALU.mult)
             out_queues[block].dma_start(out[:, block * P : (block + 1) * P], out_sb[:])

@@ -22,7 +22,8 @@ BLOCK_BANKS = BANKS // BLOCKS
 FLIPS = BANK // P
 PIECES = (128, 128, 256)
 NEG_SLOPE = 0.01
-WARM_UPS = 3
+PAIR = 2
+WARM_UPS = 4
 
 FLOPS = 2 * P * P * (ENTRIES + NODES + ENTRIES)
 
@@ -48,10 +49,13 @@ def tile_ellgat_kernel(tc, q, kw, qw, amat, offs, out):
 
         v_ps = [banks.tile([P, BANK_NODES, DEG], F32, name=f"v_ps{bank}", tag="bank") for bank in range(BANKS)]
 
-        zeros = held.tile([P, BANK], BF16, name="zeros")
-        nc.vector.memset(zeros[:], 0.0)
+        zeros = held.tile([P, P], BF16, name="zeros")
+        nc.gpsimd.memset(zeros[:], 0.0)
         for rep in range(WARM_UPS):
-            nc.tensor.matmul(v_ps[BANKS - 1][:], zeros[:, 0:P], zeros[:], start=True, stop=True)
+            nc.tensor.matmul(
+                v_ps[BANKS - 1][:], zeros[:], zeros[:].unsqueeze(1).to_broadcast([P, BANK // P, P]),
+                start=True, stop=True,
+            )
         ident = held.tile([P, P], F32, name="ident")
         make_identity(nc, ident[:])
         first_exp = held.tile([P, 1], F32, name="first_exp")
@@ -138,21 +142,23 @@ def tile_ellgat_kernel(tc, q, kw, qw, amat, offs, out):
                 out=e_sum[:], in_=e_sb[block][:].rearrange("p t h -> p h t"), axis=X_AXIS, op=ALU.add
             )
             e_inv = work.tile([P, HEADS], F32, name="e_inv")
-            for group in range(DEG // FLIPS):
-                ts = slice(group * FLIPS, (group + 1) * FLIPS)
-                ek_sb = work.tile([P, FLIPS, P], F32, name="ek_sb", bufs=BANKS)
+            for first in range(0, DEG, PAIR):
+                group, k0 = divmod(first, FLIPS)
+                ek_sb = work.tile([P, PAIR, P], F32, name="ek_sb", bufs=BLOCKS * DEG // PAIR)
                 nc.vector.tensor_tensor(
                     ek_sb[:].rearrange("p k (h o) -> p k h o", o=HEAD_F),
-                    ko_flipped[block * (DEG // FLIPS) + group][:].rearrange("p k (h o) -> p k h o", o=HEAD_F),
-                    e_sb[block][:, ts, :].unsqueeze(3).to_broadcast([P, FLIPS, HEADS, HEAD_F]),
+                    ko_flipped[block * (DEG // FLIPS) + group][:, k0 : k0 + PAIR, :].rearrange(
+                        "p k (h o) -> p k h o", o=HEAD_F
+                    ),
+                    e_sb[block][:, first : first + PAIR, :].unsqueeze(3).to_broadcast([P, PAIR, HEADS, HEAD_F]),
                     ALU.mult,
                 )
-                for k in range(FLIPS):
+                for k in range(PAIR):
                     nc.tensor.matmul(
                         out_ps[block][:], ek_sb[:, k, :], ident[:], is_transpose=True,
-                        start=(group * FLIPS + k == 0), stop=(group * FLIPS + k == DEG - 1),
+                        start=(first + k == 0), stop=(first + k == DEG - 1),
                     )
-                if group == 0:
+                if first == 0:
                     nc.vector.reciprocal(e_inv[:], e_sum[:])
                     inv_wide = work.tile([P, HEADS, HEAD_F], F32, name="inv_wide")
                     nc.scalar.activation(

@@ -15,12 +15,13 @@ HEADS = 8
 HEAD_F = P // HEADS
 ENTRIES = NODES * DEG
 BANK = 512
-BANK_NODES = BANK // DEG
-BANKS = ENTRIES // BANK
+PSUM_BANKS = 8
 BLOCKS = NODES // P
-BLOCK_BANKS = BANKS // BLOCKS
 FLIPS = BANK // P
-PIECES = (128, 128, 256)
+PIECE = NODES
+PIECE_NODES = PIECE // DEG
+PIECES = ENTRIES // PIECE
+BLOCK_PIECES = PIECES // BLOCKS
 NEG_SLOPE = 0.01
 PAIR = 2
 WARM_UPS = 4
@@ -33,8 +34,7 @@ def tile_ellgat_kernel(tc, q, kw, qw, amat, offs, out):
     with (
         tc.tile_pool(name="held", bufs=1) as held,
         tc.tile_pool(name="work", bufs=2) as work,
-        tc.psum_pool(name="banks", bufs=BANKS) as banks,
-        tc.psum_pool(name="small", bufs=BLOCKS) as small,
+        tc.psum_pool(name="banks", bufs=PSUM_BANKS) as banks,
     ):
         offsets = held.tile([P, ENTRIES // 16], U16, name="offsets")
         nc.sync.dma_start(offsets[:], offs)
@@ -47,14 +47,12 @@ def tile_ellgat_kernel(tc, q, kw, qw, amat, offs, out):
         amat_sb = held.tile([P, P], BF16, name="amat_sb")
         nc.sync.dma_start(amat_sb[:], amat)
 
-        v_ps = [banks.tile([P, BANK_NODES, DEG], F32, name=f"v_ps{bank}", tag="bank") for bank in range(BANKS)]
-
         zeros = held.tile([P, P], BF16, name="zeros")
         nc.gpsimd.memset(zeros[:], 0.0)
+        warm_ps = banks.tile([P, BANK], F32, name="warm_ps", tag="bank")
         for rep in range(WARM_UPS):
             nc.tensor.matmul(
-                v_ps[BANKS - 1][:], zeros[:], zeros[:].unsqueeze(1).to_broadcast([P, BANK // P, P]),
-                start=True, stop=True,
+                warm_ps[:], zeros[:], zeros[:].unsqueeze(1).to_broadcast([P, BANK // P, P]), start=True, stop=True
             )
         ident = held.tile([P, P], F32, name="ident")
         make_identity(nc, ident[:])
@@ -65,33 +63,28 @@ def tile_ellgat_kernel(tc, q, kw, qw, amat, offs, out):
         neg_qw = held.tile([P, P], BF16, name="neg_qw")
         nc.vector.tensor_scalar_mul(neg_qw[:], qw_sb[:], -1.0)
 
-        for bank in range(BANKS):
-            own = q_sb[:, bank * BANK_NODES : (bank + 1) * BANK_NODES]
+        v_ps = [banks.tile([P, PIECE_NODES, DEG], F32, name=f"v_ps{piece}", tag="bank") for piece in range(PIECES)]
+        for piece in range(PIECES):
+            own = q_sb[:, piece * PIECE_NODES : (piece + 1) * PIECE_NODES]
             nc.tensor.matmul(
-                v_ps[bank][:], qw_sb[:], own.unsqueeze(2).to_broadcast([P, BANK_NODES, DEG]),
+                v_ps[piece][:], qw_sb[:], own.unsqueeze(2).to_broadcast([P, PIECE_NODES, DEG]),
                 start=True, stop=False,
             )
-        for bank in range(BANKS):
-            first = 0
-            for width in PIECES:
-                entry = bank * BANK + first
-                nc.tensor.matmul(
-                    v_ps[bank][:, first // DEG : (first + width) // DEG, :],
-                    kw_sb[:],
-                    q_sb[:].indirect(offsets[:, entry // 16 : (entry + width) // 16]),
-                    start=False,
-                    stop=(first + width == BANK),
-                )
-                first += width
+        for piece in range(PIECES):
+            nc.tensor.matmul(
+                v_ps[piece][:], kw_sb[:],
+                q_sb[:].indirect(offsets[:, piece * (PIECE // 16) : (piece + 1) * (PIECE // 16)]),
+                start=False, stop=True,
+            )
 
         v_sb = held.tile([P, BLOCKS, DEG, P], F32, name="v_sb")
         x_sb = held.tile([P, BLOCKS, DEG, P], BF16, name="x_sb")
-        for bank in range(BANKS):
-            block, side = divmod(bank, BLOCK_BANKS)
-            cols = slice(side * BANK_NODES, (side + 1) * BANK_NODES)
+        for piece in range(PIECES):
+            block, side = divmod(piece, BLOCK_PIECES)
+            cols = slice(side * PIECE_NODES, (side + 1) * PIECE_NODES)
             for ts in (slice(0, DEG // 2), slice(DEG // 2, DEG)):
                 nc.scalar.activation(
-                    v_sb[:, block, ts, cols].rearrange("p t n -> p n t"), v_ps[bank][:, :, ts], ACT.Copy
+                    v_sb[:, block, ts, cols].rearrange("p t n -> p n t"), v_ps[piece][:, :, ts], ACT.Copy
                 )
                 nc.vector.scalar_tensor_tensor(
                     out=x_sb[:, block, ts, cols], in0=v_sb[:, block, ts, cols], scalar=NEG_SLOPE,
@@ -99,7 +92,7 @@ def tile_ellgat_kernel(tc, q, kw, qw, amat, offs, out):
                 )
 
         amat_heads = amat_sb[:].rearrange("p (h o) -> p o h", o=HEAD_F)[:, 0, :]
-        z_ps = [small.tile([P, P], F32, name=f"z_ps{block}", tag="z_ps") for block in range(BLOCKS)]
+        z_ps = [banks.tile([P, P], F32, name=f"z_ps{block}", tag="bank") for block in range(BLOCKS)]
         for block in range(BLOCKS):
             for t in range(DEG):
                 nc.tensor.matmul(
@@ -134,7 +127,7 @@ def tile_ellgat_kernel(tc, q, kw, qw, amat, offs, out):
                 )
                 ko_flipped.append(kt_ps)
 
-        out_ps = [small.tile([P, P], F32, name=f"out_ps{block}", tag="out_ps") for block in range(BLOCKS)]
+        out_ps = [banks.tile([P, P], F32, name=f"out_ps{block}", tag="bank") for block in range(BLOCKS)]
         inv_flipped = []
         for block in range(BLOCKS):
             e_sum = work.tile([P, HEADS], F32, name="e_sum")
@@ -164,7 +157,7 @@ def tile_ellgat_kernel(tc, q, kw, qw, amat, offs, out):
                     nc.scalar.activation(
                         inv_wide[:], e_inv[:].unsqueeze(2).to_broadcast([P, HEADS, HEAD_F]), ACT.Copy
                     )
-                    inv_ps = small.tile([P, P], F32, name=f"inv_ps{block}", tag="z_ps")
+                    inv_ps = banks.tile([P, P], F32, name=f"inv_ps{block}", tag="bank")
                     nc.tensor.transpose(inv_ps[:], inv_wide[:].rearrange("p h o -> p (h o)"), ident[:])
                     inv_sb = work.tile([P, P], F32, name="inv_sb")
                     nc.scalar.activation(inv_sb[:], inv_ps[:], ACT.Copy)

@@ -23,6 +23,7 @@ PIECE_NODES = PIECE // DEG
 PIECES = ENTRIES // PIECE
 BLOCK_PIECES = PIECES // BLOCKS
 NEG_SLOPE = 0.01
+COPIES = BANK // (DEG * HEADS)
 PAIR = 2
 WARM_UPS = 4
 
@@ -91,23 +92,21 @@ def tile_ellgat_kernel(tc, q, kw, qw, amat, offs, out):
                     in1=v_sb[:, block, ts, cols], op0=ALU.mult, op1=ALU.max,
                 )
 
-        amat_heads = amat_sb[:].rearrange("p (h o) -> p o h", o=HEAD_F)[:, 0, :]
-        z_ps = [banks.tile([P, P], F32, name=f"z_ps{block}", tag="bank") for block in range(BLOCKS)]
+        amat_heads = amat_sb[:].rearrange("p (h o) -> p h o", o=HEAD_F)[:, :, 0:COPIES]
+        z_ps = [banks.tile([P, DEG, HEADS, COPIES], F32, name=f"z_ps{block}", tag="bank") for block in range(BLOCKS)]
         for block in range(BLOCKS):
             for t in range(DEG):
-                nc.tensor.matmul(
-                    z_ps[block][:, t * HEADS : (t + 1) * HEADS], x_sb[:, block, t, :], amat_heads, start=True, stop=True
-                )
+                nc.tensor.matmul(z_ps[block][:, t, :, :], x_sb[:, block, t, :], amat_heads, start=True, stop=True)
 
         e_sb = [held.tile([P, DEG, HEADS], F32, name=f"e_sb{block}") for block in range(BLOCKS)]
         for block in range(BLOCKS):
             z_max = work.tile([P, HEADS], F32, name="z_max")
             nc.vector.tensor_reduce(
-                out=z_max[:], in_=z_ps[block][:, 0:DEG * HEADS].rearrange("p (t h) -> p h t", h=HEADS),
+                out=z_max[:], in_=z_ps[block][:, :, :, 0].rearrange("p t h -> p h t"),
                 axis=X_AXIS, op=ALU.max,
             )
             nc.vector.tensor_tensor(
-                e_sb[block][:], z_ps[block][:, 0:DEG * HEADS].rearrange("p (t h) -> p t h", h=HEADS),
+                e_sb[block][:], z_ps[block][:, :, :, 0],
                 z_max[:].unsqueeze(1).to_broadcast([P, DEG, HEADS]), ALU.subtract,
             )
             nc.scalar.activation(e_sb[block][:], e_sb[block][:], ACT.Exp)
@@ -158,7 +157,9 @@ def tile_ellgat_kernel(tc, q, kw, qw, amat, offs, out):
                         inv_wide[:], e_inv[:].unsqueeze(2).to_broadcast([P, HEADS, HEAD_F]), ACT.Copy
                     )
                     inv_ps = banks.tile([P, P], F32, name=f"inv_ps{block}", tag="bank")
-                    nc.tensor.transpose(inv_ps[:], inv_wide[:].rearrange("p h o -> p (h o)"), ident[:])
+                    nc.tensor.matmul(
+                        inv_ps[:], inv_wide[:].rearrange("p h o -> p (h o)"), ident[:], start=True, stop=True
+                    )
                     inv_sb = work.tile([P, P], F32, name="inv_sb")
                     nc.scalar.activation(inv_sb[:], inv_ps[:], ACT.Copy)
                     inv_flipped.append(inv_sb)

@@ -157,9 +157,7 @@ def tile_ellgat_kernel(tc, q, kw, qw, amat, offs, out):
                         inv_wide[:], e_inv[:].unsqueeze(2).to_broadcast([P, HEADS, HEAD_F]), ACT.Copy
                     )
                     inv_ps = banks.tile([P, P], F32, name=f"inv_ps{block}", tag="bank")
-                    nc.tensor.matmul(
-                        inv_ps[:], inv_wide[:].rearrange("p h o -> p (h o)"), ident[:], start=True, stop=True
-                    )
+                    nc.tensor.transpose(inv_ps[:], inv_wide[:].rearrange("p h o -> p (h o)"), ident[:])
                     inv_sb = work.tile([P, P], F32, name="inv_sb")
                     nc.scalar.activation(inv_sb[:], inv_ps[:], ACT.Copy)
                     inv_flipped.append(inv_sb)

@@ -57,9 +57,6 @@ def tile_ellgat_kernel(tc, q, kw, qw, amat, offs, out):
             )
         ident = held.tile([P, P], F32, name="ident")
         make_identity(nc, ident[:])
-        first_exp = held.tile([P, 1], F32, name="first_exp")
-        nc.vector.memset(first_exp[:], 0.0)
-        nc.scalar.activation(first_exp[:], first_exp[:], ACT.Exp)
 
         neg_qw = held.tile([P, P], BF16, name="neg_qw")
         nc.vector.tensor_scalar_mul(neg_qw[:], qw_sb[:], -1.0)

@@ -24,7 +24,7 @@ PIECES = ENTRIES // PIECE
 BLOCK_PIECES = PIECES // BLOCKS
 NEG_SLOPE = 0.01
 COPIES = BANK // (DEG * HEADS)
-PAIR = 2
+PAIR = 1
 WARM_UPS = 4
 
 FLOPS = 2 * P * P * (ENTRIES + NODES + ENTRIES)

@@ -159,7 +159,7 @@ def tile_ellgat_kernel(tc, q, kw, qw, amat, offs, out):
                     nc.scalar.activation(inv_sb[:], inv_ps[:], ACT.Copy)
                     inv_flipped.append(inv_sb)
 
-        out_queues = (nc.sync, nc.scalar)
+        out_queues = (nc.scalar, nc.sync)
         for block in range(BLOCKS):
             out_sb = work.tile([P, P], F32, name="out_sb")
             nc.vector.tensor_tensor(out_sb[:], out_ps[block][:], inv_flipped[block][:], ALU.mult)

@@ -91,9 +91,34 @@ def tile_ellgat_kernel(tc, q, kw, qw, amat, offs, out):
 
         amat_heads = amat_sb[:].rearrange("p (h o) -> p h o", o=HEAD_F)[:, :, 0:COPIES]
         z_ps = [banks.tile([P, DEG, HEADS, COPIES], F32, name=f"z_ps{block}", tag="bank") for block in range(BLOCKS)]
-        for block in range(BLOCKS):
+
+        def logits(block):
             for t in range(DEG):
                 nc.tensor.matmul(z_ps[block][:, t, :, :], x_sb[:, block, t, :], amat_heads, start=True, stop=True)
+
+        ko_flipped = [
+            [banks.tile([P, FLIPS, P], F32, name=f"kt_ps{block}{group}", tag="bank") for group in range(DEG // FLIPS)]
+            for block in range(BLOCKS)
+        ]
+
+        def open_ko(block):
+            for kt_ps in ko_flipped[block]:
+                nc.tensor.matmul(
+                    kt_ps[:], q_sb[:, block * P : (block + 1) * P],
+                    neg_qw[:].unsqueeze(1).to_broadcast([P, FLIPS, P]), start=True, stop=False,
+                )
+
+        def close_ko(block):
+            for group, kt_ps in enumerate(ko_flipped[block]):
+                for k in range(FLIPS):
+                    nc.tensor.matmul(
+                        kt_ps[:, k, :], v_sb[:, block, group * FLIPS + k, :], ident[:], is_transpose=True,
+                        start=False, stop=(k == FLIPS - 1),
+                    )
+
+        logits(0)
+        open_ko(0)
+        logits(1)
 
         e_sb = [held.tile([P, DEG, HEADS], F32, name=f"e_sb{block}") for block in range(BLOCKS)]
         for block in range(BLOCKS):
@@ -108,20 +133,9 @@ def tile_ellgat_kernel(tc, q, kw, qw, amat, offs, out):
             )
             nc.scalar.activation(e_sb[block][:], e_sb[block][:], ACT.Exp)
 
-        ko_flipped = []
-        for block in range(BLOCKS):
-            for group in range(DEG // FLIPS):
-                kt_ps = banks.tile([P, FLIPS, P], F32, name=f"kt_ps{block}{group}", tag="bank")
-                for k in range(FLIPS):
-                    nc.tensor.matmul(
-                        kt_ps[:, k, :], v_sb[:, block, group * FLIPS + k, :], ident[:], is_transpose=True,
-                        start=(k == 0), stop=False,
-                    )
-                nc.tensor.matmul(
-                    kt_ps[:], q_sb[:, block * P : (block + 1) * P],
-                    neg_qw[:].unsqueeze(1).to_broadcast([P, FLIPS, P]), start=False, stop=True,
-                )
-                ko_flipped.append(kt_ps)
+        close_ko(0)
+        open_ko(1)
+        close_ko(1)
 
         out_ps = [banks.tile([P, P], F32, name=f"out_ps{block}", tag="bank") for block in range(BLOCKS)]
         inv_flipped = []
@@ -136,7 +150,7 @@ def tile_ellgat_kernel(tc, q, kw, qw, amat, offs, out):
                 ek_sb = work.tile([P, PAIR, P], F32, name="ek_sb", bufs=BLOCKS * DEG // PAIR)
                 nc.vector.tensor_tensor(
                     ek_sb[:].rearrange("p k (h o) -> p k h o", o=HEAD_F),
-                    ko_flipped[block * (DEG // FLIPS) + group][:, k0 : k0 + PAIR, :].rearrange(
+                    ko_flipped[block][group][:, k0 : k0 + PAIR, :].rearrange(
                         "p k (h o) -> p k h o", o=HEAD_F
                     ),
                     e_sb[block][:, first : first + PAIR, :].unsqueeze(3).to_broadcast([P, PAIR, HEADS, HEAD_F]),

@@ -82,7 +82,7 @@ def tile_ellgat_kernel(tc, q, kw, qw, amat, offs, out):
             cols = slice(side * PIECE_NODES, (side + 1) * PIECE_NODES)
             for ts in (slice(0, DEG // 2), slice(DEG // 2, DEG)):
                 nc.scalar.activation(
-                    v_sb[:, block, ts, cols].rearrange("p t n -> p n t"), v_ps[piece][:, :, ts], ACT.Copy
+                    v_sb[:, block, ts, cols], v_ps[piece][:, :, ts].rearrange("p n t -> p t n"), ACT.Copy
                 )
                 nc.vector.scalar_tensor_tensor(
                     out=x_sb[:, block, ts, cols], in0=v_sb[:, block, ts, cols], scalar=NEG_SLOPE,

@@ -25,7 +25,7 @@ BLOCK_PIECES = PIECES // BLOCKS
 NEG_SLOPE = 0.01
 COPIES = BANK // (DEG * HEADS)
 PAIR = 1
-WARM_UPS = 4
+WARM_UPS = 3
 
 FLOPS = 2 * P * P * (ENTRIES + NODES + ENTRIES)
 
@@ -37,14 +37,14 @@ def tile_ellgat_kernel(tc, q, kw, qw, amat, offs, out):
         tc.tile_pool(name="work", bufs=2) as work,
         tc.psum_pool(name="banks", bufs=PSUM_BANKS) as banks,
     ):
-        offsets = held.tile([P, ENTRIES // 16], U16, name="offsets")
-        nc.sync.dma_start(offsets[:], offs)
         q_sb = held.tile([P, NODES], BF16, name="q_sb")
-        nc.scalar.dma_start(q_sb[:], q)
-        kw_sb = held.tile([P, P], BF16, name="kw_sb")
-        nc.sync.dma_start(kw_sb[:], kw)
+        nc.sync.dma_start(q_sb[:], q)
         qw_sb = held.tile([P, P], BF16, name="qw_sb")
         nc.scalar.dma_start(qw_sb[:], qw)
+        offsets = held.tile([P, ENTRIES // 16], U16, name="offsets")
+        nc.sync.dma_start(offsets[:], offs)
+        kw_sb = held.tile([P, P], BF16, name="kw_sb")
+        nc.scalar.dma_start(kw_sb[:], kw)
         amat_sb = held.tile([P, P], BF16, name="amat_sb")
         nc.sync.dma_start(amat_sb[:], amat)
 

@@ -25,6 +25,7 @@ BLOCK_PIECES = PIECES // BLOCKS
 NEG_SLOPE = 0.01
 COPIES = BANK // (DEG * HEADS)
 PAIR = 1
+ZEROS = 16
 WARM_UPS = 3
 
 FLOPS = 2 * P * P * (ENTRIES + NODES + ENTRIES)
@@ -48,12 +49,13 @@ def tile_ellgat_kernel(tc, q, kw, qw, amat, offs, out):
         amat_sb = held.tile([P, P], BF16, name="amat_sb")
         nc.sync.dma_start(amat_sb[:], amat)
 
-        zeros = held.tile([P, P], BF16, name="zeros")
+        zeros = held.tile([P, ZEROS], BF16, name="zeros")
         nc.gpsimd.memset(zeros[:], 0.0)
         warm_ps = banks.tile([P, BANK], F32, name="warm_ps", tag="bank")
         for rep in range(WARM_UPS):
             nc.tensor.matmul(
-                warm_ps[:], zeros[:], zeros[:].unsqueeze(1).to_broadcast([P, BANK // P, P]), start=True, stop=True
+                warm_ps[:], zeros[:, 0:1].to_broadcast([P, P]), zeros[:, 0:1].to_broadcast([P, BANK]),
+                start=True, stop=True,
             )
         ident = held.tile([P, P], F32, name="ident")
         make_identity(nc, ident[:])

@@ -24,7 +24,7 @@ PIECES = ENTRIES // PIECE
 BLOCK_PIECES = PIECES // BLOCKS
 NEG_SLOPE = 0.01
 COPIES = BANK // (DEG * HEADS)
-PAIR = 1
+COUNTS = (2, 1)
 ZEROS = 16
 WARM_UPS = 3
 
@@ -147,18 +147,19 @@ def tile_ellgat_kernel(tc, q, kw, qw, amat, offs, out):
                 out=e_sum[:], in_=e_sb[block][:].rearrange("p t h -> p h t"), axis=X_AXIS, op=ALU.add
             )
             e_inv = work.tile([P, HEADS], F32, name="e_inv")
-            for first in range(0, DEG, PAIR):
+            count = COUNTS[block]
+            for first in range(0, DEG, count):
                 group, k0 = divmod(first, FLIPS)
-                ek_sb = work.tile([P, PAIR, P], F32, name="ek_sb", bufs=BLOCKS * DEG // PAIR)
+                ek_sb = work.tile([P, count, P], F32, name="ek_sb", bufs=BLOCKS * DEG)
                 nc.vector.tensor_tensor(
                     ek_sb[:].rearrange("p k (h o) -> p k h o", o=HEAD_F),
-                    ko_flipped[block][group][:, k0 : k0 + PAIR, :].rearrange(
+                    ko_flipped[block][group][:, k0 : k0 + count, :].rearrange(
                         "p k (h o) -> p k h o", o=HEAD_F
                     ),
-                    e_sb[block][:, first : first + PAIR, :].unsqueeze(3).to_broadcast([P, PAIR, HEADS, HEAD_F]),
+                    e_sb[block][:, first : first + count, :].unsqueeze(3).to_broadcast([P, count, HEADS, HEAD_F]),
                     ALU.mult,
                 )
-                for k in range(PAIR):
+                for k in range(count):
                     nc.tensor.matmul(
                         out_ps[block][:], ek_sb[:, k, :], ident[:], is_transpose=True,
                         start=(first + k == 0), stop=(first + k == DEG - 1),

import concourse.mybir as mybir
from concourse.masks import make_identity

F32 = mybir.dt.float32
BF16 = mybir.dt.bfloat16
U16 = mybir.dt.uint16
ALU = mybir.AluOpType
ACT = mybir.ActivationFunctionType
X_AXIS = mybir.AxisListType.X

P = 128
NODES = 256
DEG = 8
HEADS = 8
HEAD_F = P // HEADS
ENTRIES = NODES * DEG
BANK = 512
PSUM_BANKS = 8
BLOCKS = NODES // P
FLIPS = BANK // P
PIECE = NODES
PIECE_NODES = PIECE // DEG
PIECES = ENTRIES // PIECE
BLOCK_PIECES = PIECES // BLOCKS
NEG_SLOPE = 0.01
COPIES = BANK // (DEG * HEADS)
COUNTS = (2, 1)
ZEROS = 16
WARM_UPS = 3

FLOPS = 2 * P * P * (ENTRIES + NODES + ENTRIES)


def tile_ellgat_kernel(tc, q, kw, qw, amat, offs, out):
    nc = tc.nc
    with (
        tc.tile_pool(name="held", bufs=1) as held,
        tc.tile_pool(name="work", bufs=2) as work,
        tc.psum_pool(name="banks", bufs=PSUM_BANKS) as banks,
    ):
        q_sb = held.tile([P, NODES], BF16, name="q_sb")
        nc.sync.dma_start(q_sb[:], q)
        qw_sb = held.tile([P, P], BF16, name="qw_sb")
        nc.scalar.dma_start(qw_sb[:], qw)
        offsets = held.tile([P, ENTRIES // 16], U16, name="offsets")
        nc.sync.dma_start(offsets[:], offs)
        kw_sb = held.tile([P, P], BF16, name="kw_sb")
        nc.scalar.dma_start(kw_sb[:], kw)
        amat_sb = held.tile([P, P], BF16, name="amat_sb")
        nc.sync.dma_start(amat_sb[:], amat)

        zeros = held.tile([P, ZEROS], BF16, name="zeros")
        nc.gpsimd.memset(zeros[:], 0.0)
        warm_ps = banks.tile([P, BANK], F32, name="warm_ps", tag="bank")
        for rep in range(WARM_UPS):
            nc.tensor.matmul(
                warm_ps[:], zeros[:, 0:1].to_broadcast([P, P]), zeros[:, 0:1].to_broadcast([P, BANK]),
                start=True, stop=True,
            )
        ident = held.tile([P, P], F32, name="ident")
        make_identity(nc, ident[:])

        neg_qw = held.tile([P, P], BF16, name="neg_qw")
        nc.vector.tensor_scalar_mul(neg_qw[:], qw_sb[:], -1.0)

        v_ps = [banks.tile([P, PIECE_NODES, DEG], F32, name=f"v_ps{piece}", tag="bank") for piece in range(PIECES)]
        for piece in range(PIECES):
            own = q_sb[:, piece * PIECE_NODES : (piece + 1) * PIECE_NODES]
            nc.tensor.matmul(
                v_ps[piece][:], qw_sb[:], own.unsqueeze(2).to_broadcast([P, PIECE_NODES, DEG]),
                start=True, stop=False,
            )
        for piece in range(PIECES):
            nc.tensor.matmul(
                v_ps[piece][:], kw_sb[:],
                q_sb[:].indirect(offsets[:, piece * (PIECE // 16) : (piece + 1) * (PIECE // 16)]),
                start=False, stop=True,
            )

        v_sb = held.tile([P, BLOCKS, DEG, P], F32, name="v_sb")
        x_sb = held.tile([P, BLOCKS, DEG, P], BF16, name="x_sb")
        for piece in range(PIECES):
            block, side = divmod(piece, BLOCK_PIECES)
            cols = slice(side * PIECE_NODES, (side + 1) * PIECE_NODES)
            for ts in (slice(0, DEG // 2), slice(DEG // 2, DEG)):
                nc.scalar.activation(
                    v_sb[:, block, ts, cols], v_ps[piece][:, :, ts].rearrange("p n t -> p t n"), ACT.Copy
                )
                nc.vector.scalar_tensor_tensor(
                    out=x_sb[:, block, ts, cols], in0=v_sb[:, block, ts, cols], scalar=NEG_SLOPE,
                    in1=v_sb[:, block, ts, cols], op0=ALU.mult, op1=ALU.max,
                )

        amat_heads = amat_sb[:].rearrange("p (h o) -> p h o", o=HEAD_F)[:, :, 0:COPIES]
        z_ps = [banks.tile([P, DEG, HEADS, COPIES], F32, name=f"z_ps{block}", tag="bank") for block in range(BLOCKS)]

        def logits(block):
            for t in range(DEG):
                nc.tensor.matmul(z_ps[block][:, t, :, :], x_sb[:, block, t, :], amat_heads, start=True, stop=True)

        ko_flipped = [
            [banks.tile([P, FLIPS, P], F32, name=f"kt_ps{block}{group}", tag="bank") for group in range(DEG // FLIPS)]
            for block in range(BLOCKS)
        ]

        def open_ko(block):
            for kt_ps in ko_flipped[block]:
                nc.tensor.matmul(
                    kt_ps[:], q_sb[:, block * P : (block + 1) * P],
                    neg_qw[:].unsqueeze(1).to_broadcast([P, FLIPS, P]), start=True, stop=False,
                )

        def close_ko(block):
            for group, kt_ps in enumerate(ko_flipped[block]):
                for k in range(FLIPS):
                    nc.tensor.matmul(
                        kt_ps[:, k, :], v_sb[:, block, group * FLIPS + k, :], ident[:], is_transpose=True,
                        start=False, stop=(k == FLIPS - 1),
                    )

        logits(0)
        open_ko(0)
        logits(1)

        e_sb = [held.tile([P, DEG, HEADS], F32, name=f"e_sb{block}") for block in range(BLOCKS)]
        for block in range(BLOCKS):
            z_max = work.tile([P, HEADS], F32, name="z_max")
            nc.vector.tensor_reduce(
                out=z_max[:], in_=z_ps[block][:, :, :, 0].rearrange("p t h -> p h t"),
                axis=X_AXIS, op=ALU.max,
            )
            nc.vector.tensor_tensor(
                e_sb[block][:], z_ps[block][:, :, :, 0],
                z_max[:].unsqueeze(1).to_broadcast([P, DEG, HEADS]), ALU.subtract,
            )
            nc.scalar.activation(e_sb[block][:], e_sb[block][:], ACT.Exp)

        close_ko(0)
        open_ko(1)
        close_ko(1)

        out_ps = [banks.tile([P, P], F32, name=f"out_ps{block}", tag="bank") for block in range(BLOCKS)]
        inv_flipped = []
        for block in range(BLOCKS):
            e_sum = work.tile([P, HEADS], F32, name="e_sum")
            nc.vector.tensor_reduce(
                out=e_sum[:], in_=e_sb[block][:].rearrange("p t h -> p h t"), axis=X_AXIS, op=ALU.add
            )
            e_inv = work.tile([P, HEADS], F32, name="e_inv")
            count = COUNTS[block]
            for first in range(0, DEG, count):
                group, k0 = divmod(first, FLIPS)
                ek_sb = work.tile([P, count, P], F32, name="ek_sb", bufs=BLOCKS * DEG)
                nc.vector.tensor_tensor(
                    ek_sb[:].rearrange("p k (h o) -> p k h o", o=HEAD_F),
                    ko_flipped[block][group][:, k0 : k0 + count, :].rearrange(
                        "p k (h o) -> p k h o", o=HEAD_F
                    ),
                    e_sb[block][:, first : first + count, :].unsqueeze(3).to_broadcast([P, count, HEADS, HEAD_F]),
                    ALU.mult,
                )
                for k in range(count):
                    nc.tensor.matmul(
                        out_ps[block][:], ek_sb[:, k, :], ident[:], is_transpose=True,
                        start=(first + k == 0), stop=(first + k == DEG - 1),
                    )
                if first == 0:
                    nc.vector.reciprocal(e_inv[:], e_sum[:])
                    inv_wide = work.tile([P, HEADS, HEAD_F], F32, name="inv_wide")
                    nc.scalar.activation(
                        inv_wide[:], e_inv[:].unsqueeze(2).to_broadcast([P, HEADS, HEAD_F]), ACT.Copy
                    )
                    inv_ps = banks.tile([P, P], F32, name=f"inv_ps{block}", tag="bank")
                    nc.tensor.transpose(inv_ps[:], inv_wide[:].rearrange("p h o -> p (h o)"), ident[:])
                    inv_sb = work.tile([P, P], F32, name="inv_sb")
                    nc.scalar.activation(inv_sb[:], inv_ps[:], ACT.Copy)
                    inv_flipped.append(inv_sb)

        out_queues = (nc.scalar, nc.sync)
        for block in range(BLOCKS):
            out_sb = work.tile([P, P], F32, name="out_sb")
            nc.vector.tensor_tensor(out_sb[:], out_ps[block][:], inv_flipped[block][:], ALU.mult)
            out_queues[block].dma_start(out[:, block * P : (block + 1) * P], out_sb[:])
